import numpy as np
import ml_dtypes


def mxq(x, axis, fmt="e4m3"):
    dtype, down = {"e4m3": (ml_dtypes.float8_e4m3fn, 7), "e5m2": (ml_dtypes.float8_e5m2, 14)}[fmt]
    v = np.moveaxis(np.asarray(x, np.float32).astype(ml_dtypes.bfloat16).astype(np.float64), axis, -1)
    blocks = v.reshape(v.shape[:-1] + (-1, 32))
    amax = np.abs(blocks).max(-1, keepdims=True)
    byte = np.maximum(np.where(amax > 0, np.frexp(amax)[1] - 1 + 127, 0) - down, 1)
    scale = np.exp2(byte - 127.0)
    codes = (blocks / scale).astype(np.float32).astype(dtype).astype(np.float64)
    return np.moveaxis((codes * scale).reshape(v.shape), -1, axis)


WIDE = False


def mx_kscale(k):
    if not WIDE:
        return np.ones(k)
    levels = np.array([20, -20, 10, -10, 0])
    a = np.random.permutation(np.resize(levels, k // 512 * 4)).reshape(k // 512, 4)
    idx = np.arange(k)
    return np.exp2(a[idx // 512, idx % 128 // 32])


BF16 = ml_dtypes.bfloat16


def bf(x):
    return np.asarray(x, np.float32).astype(BF16)


def f64(x):
    return np.asarray(x).astype(np.float64)


E, I, O, N = 2, 1024, 2048, 512
C = E


def setup_inputs():
    s = mx_kscale(C * N).reshape(C, N)
    inputs = np.random.standard_normal((C, O, N)) * s[:, None, :]
    weight = np.random.uniform(0.0, 1.0, (E, I, O)) * 1.7 / np.sqrt(O)
    g = np.random.standard_normal((C, E, I, N)) * np.exp2(np.random.randint(-12, 1, (C, E, 1, N))) / s[:, None, None, :]
    return {"inputs": bf(inputs), "weight": bf(weight), "expert_size": E,
            "grad_out": bf(g.reshape(C * E, I, N))}


def reference(inputs, weight, expert_size, grad_out):
    num_experts = weight.shape[0]
    rows = weight.shape[1]
    chunks = f64(inputs)[:num_experts]
    c, o, n = chunks.shape
    g = f64(grad_out).reshape(c, num_experts, rows, n)
    gk = g.transpose(1, 2, 0, 3).reshape(num_experts, rows, c * n)
    xk = chunks.transpose(1, 0, 2).reshape(o, c * n)
    gq = mxq(gk, 2, "e5m2")
    xq = mxq(xk, 1, "e4m3")
    return gq @ xq.T

@@ -1,0 +1,193 @@
+from contextlib import ExitStack
+
+import concourse.mybir as mybir
+from concourse.masks import make_identity
+
+F32 = mybir.dt.float32
+BF16 = mybir.dt.bfloat16
+U32 = mybir.dt.uint32
+U8 = mybir.dt.uint8
+E4M3X4 = mybir.dt.float8_e4m3fn_x4
+E5M2X4 = mybir.dt.float8_e5m2_x4
+
+P = 128
+C = 2
+E = 2
+I = 1024
+O = 2048
+N = 512
+NT = 512
+
+FLOPS = 2 * E * I * O * C * N
+BYTES = 2 * (C * O * N + C * E * I * N) + 4 * E * I * O
+
+
+def tile_flaxparallelexperts_kernel(tc, inputs, weight, expert_size, grad_out, out):
+    nc = tc.nc
+    with ExitStack() as ctx:
+        const = ctx.enter_context(tc.tile_pool(name="const", bufs=1))
+        rawp = ctx.enter_context(tc.tile_pool(name="raw", bufs=1))
+        grpp = ctx.enter_context(tc.tile_pool(name="grp", bufs=4))
+        keep = ctx.enter_context(tc.tile_pool(name="keep", bufs=1))
+        stgp = ctx.enter_context(tc.tile_pool(name="stg", bufs=8))
+        psum = ctx.enter_context(tc.psum_pool(name="psum", bufs=8))
+        ctx.enter_context(tc.manual_schedule())
+
+        raw = {}
+        codes = {}
+        scales = {}
+
+        def load_x(c, ch):
+            t = rawp.tile([P, 4 * N], BF16, name="xr%d%d" % (c, ch))
+            nc.sync.dma_start(
+                out=t[:],
+                in_=inputs[c, ch * 512 : (ch + 1) * 512, :].rearrange("(p t) n -> p (t n)", t=4),
+            )
+            raw[("X", c, ch)] = t[:].bitcast(F32)
+
+        def load_g_half(c, e, h):
+            t = rawp.tile([P, 4 * N], BF16, name="gr%d%d%d" % (c, e, h))
+            nc.sync.dma_start(
+                out=t[:],
+                in_=grad_out[c * E + e].rearrange("(p t) n -> p (t n)", t=8)[:, h * 4 * N : (h + 1) * 4 * N],
+            )
+            raw[("G", c, e, h)] = t[:].bitcast(F32)
+
+        def load_g_whole(c, e):
+            t = rawp.tile([P, 8 * N], BF16, name="gr%d%d" % (c, e))
+            nc.sync.dma_start(out=t[:], in_=grad_out[c * E + e].rearrange("(p t) n -> p (t n)", t=8))
+            for h in range(2):
+                raw[("G", c, e, h)] = t[:].bitcast(F32)[:, h * 2 * N : (h + 1) * 2 * N]
+
+        load_x(0, 0)
+        load_x(1, 0)
+        load_g_half(0, 0, 0)
+        load_g_half(1, 0, 0)
+        for ch in range(1, 4):
+            load_x(0, ch)
+            load_x(1, ch)
+        load_g_half(0, 0, 1)
+        load_g_half(1, 0, 1)
+        load_g_whole(0, 1)
+        load_g_whole(1, 1)
+
+        ident = const.tile([P, P], F32, name="ident")
+        make_identity(nc, ident[:])
+        warm_in = const.tile([P, 8], F32, name="warm_in")
+        warm_out = const.tile([P, 8], F32, name="warm_out")
+        nc.vector.memset(warm_in[:], 0.0)
+        nc.scalar.copy(out=warm_out[:], in_=warm_in[:])
+
+        def quantise(u, grp):
+            nm = u[0] + ("%d" * (len(u) - 1)) % tuple(u[1:])
+            cd = keep.tile([P, NT], U32, name="cd" + nm, align_bytes=64)
+            sc = keep.tile([P, NT], U8, name="sc" + nm, align_bytes=64)
+            nc.vector.quantize_mx(
+                out=cd[:].bitcast(E4M3X4 if u[0] == "X" else E5M2X4),
+                scales=sc[:],
+                in_=grp[:],
+            )
+            codes[u] = cd
+            scales[u] = sc
+
+        def transposes(units, quantise_each):
+            grps = []
+            for u in units:
+                grp = grpp.tile([P, 4 * NT], BF16, name="grp", tag="grp", align_bytes=64)
+                grp_w = grp[:].bitcast(F32)
+                for b in range(2):
+                    tp = psum.tile([P, NT], F32, name="tp", tag="bank")
+                    for j in range(4):
+                        nc.tensor.transpose(
+                            out=tp[:, j * P : (j + 1) * P],
+                            in_=raw[u][:, (4 * b + j) * P : (4 * b + j + 1) * P],
+                            identity=ident[:],
+                        )
+                    dst = grp_w[:, b * NT : (b + 1) * NT].rearrange("k (t p u) -> k t p u", t=2, u=2)
+                    src = tp[:].rearrange("k (t u p) -> k t p u", t=2, u=2)
+                    if b == 0:
+                        nc.vector.tensor_copy(out=dst, in_=src)
+                    else:
+                        nc.scalar.copy(out=dst, in_=src)
+                if quantise_each:
+                    quantise(u, grp)
+                else:
+                    grps.append((u, grp))
+            for u, grp in grps:
+                quantise(u, grp)
+
+        first = [const.tile([P, 4, 2 * NT], F32, name="first%d" % half) for half in range(2)]
+        stage = {}
+
+        def stage_of(e, t, ch):
+            if e == 0 and t < 4:
+                return first[ch // 2][:, t, (ch % 2) * NT : (ch % 2 + 1) * NT]
+            if (e, t) not in stage:
+                stage[(e, t)] = stgp.tile([P, O], F32, name="stg", tag="stg")
+            return stage[(e, t)][:, ch * NT : (ch + 1) * NT]
+
+        def products(tiles, pattern, chunk_major):
+            accs = [psum.tile([P, NT], F32, name="acc", tag="bank") for tl in tiles]
+            if chunk_major:
+                order = [(c, k) for c in range(C) for k in range(len(tiles))]
+            else:
+                order = [(c, k) for k in range(len(tiles)) for c in range(C)]
+            for c, k in order:
+                e, t, ch = tiles[k]
+                g = ("G", c, e, t // 4)
+                x = ("X", c, ch)
+                cols = slice((t % 4) * P, (t % 4 + 1) * P)
+                nc.tensor.matmul_mx(
+                    out=accs[k][:],
+                    lhsT=codes[g][:, cols].bitcast(E5M2X4),
+                    lhsT_scale=scales[g][:, cols],
+                    rhs=codes[x][:].bitcast(E4M3X4),
+                    rhs_scale=scales[x][:],
+                    start=(c == 0),
+                    stop=(c == C - 1),
+                )
+            for k, (e, t, ch) in enumerate(tiles):
+                dst = stage_of(e, t, ch).rearrange("i (p t) -> i p t", t=4)
+                src = accs[k][:].rearrange("i (t p) -> i p t", t=4)
+                if pattern[k] == "A":
+                    nc.scalar.copy(out=dst, in_=src)
+                else:
+                    nc.vector.tensor_copy(out=dst, in_=src)
+
+        out_v = [out[e].rearrange("(p t) o -> p t o", t=8) for e in range(E)]
+
+        def column_quad(e, h, ch):
+            return [(e, 4 * h + tt, ch) for tt in range(4)]
+
+        def row_quad(e, t):
+            return [(e, t, ch) for ch in range(4)]
+
+        transposes([("X", 0, 0)], True)
+        transposes([("X", 1, 0)], True)
+        transposes([("G", 0, 0, 0)], True)
+        transposes([("G", 1, 0, 0)], True)
+        products(column_quad(0, 0, 0), "ADAA", True)
+        transposes([("X", 0, 1), ("X", 1, 1)], False)
+        transposes([("X", 0, 2), ("X", 1, 2)], False)
+        products(column_quad(0, 0, 1), "ADAA", True)
+        nc.sync.dma_start(out=out_v[0][:, 0:4, 0:1024], in_=first[0][:])
+        transposes([("X", 0, 3), ("X", 1, 3)], False)
+        products(column_quad(0, 0, 2), "ADAA", True)
+        transposes([("G", 0, 0, 1), ("G", 1, 0, 1)], False)
+        products(column_quad(0, 0, 3), "ADAA", True)
+        nc.sync.dma_start(out=out_v[0][:, 0:4, 1024:2048], in_=first[1][:])
+
+        rows = [(0, t) for t in range(4, 8)] + [(1, t) for t in range(8)]
+        for e, t in rows:
+            last = (e, t) == rows[-1]
+            products(row_quad(e, t), "ADAD", not last)
+            st = stage[(e, t)]
+            if last:
+                nc.sync.dma_start(out=out_v[e][:, t, 0:1024], in_=st[:, 0:1024])
+                nc.sync.dma_start(out=out_v[e][:, t, 1024:2048], in_=st[:, 1024:2048])
+            else:
+                nc.sync.dma_start(out=out_v[e][:, t, :], in_=st[:])
+            if (e, t) == (0, 5):
+                transposes([("G", 0, 1, 0), ("G", 1, 1, 0)], False)
+            if (e, t) == (1, 1):
+                transposes([("G", 0, 1, 1), ("G", 1, 1, 1)], False)

@@ -169,24 +169,25 @@ def tile_flaxparallelexperts_kernel(tc, inputs, weight, expert_size, grad_out, o
         products(column_quad(0, 0, 0), "ADAA", True)
         transposes([("X", 0, 1), ("X", 1, 1)], False)
         transposes([("X", 0, 2), ("X", 1, 2)], False)
-        products(column_quad(0, 0, 1), "ADAA", True)
+        products(column_quad(0, 0, 1), "ADAA", False)
         nc.sync.dma_start(out=out_v[0][:, 0:4, 0:1024], in_=first[0][:])
         transposes([("X", 0, 3), ("X", 1, 3)], False)
-        products(column_quad(0, 0, 2), "ADAA", True)
+        products(column_quad(0, 0, 2), "ADAA", False)
         transposes([("G", 0, 0, 1), ("G", 1, 0, 1)], False)
-        products(column_quad(0, 0, 3), "ADAA", True)
+        products(column_quad(0, 0, 3), "ADAA", False)
         nc.sync.dma_start(out=out_v[0][:, 0:4, 1024:2048], in_=first[1][:])
 
         rows = [(0, t) for t in range(4, 8)] + [(1, t) for t in range(8)]
         for e, t in rows:
-            last = (e, t) == rows[-1]
-            products(row_quad(e, t), "ADAD", not last)
+            products(row_quad(e, t), "ADAD", False)
             st = stage[(e, t)]
-            if last:
-                nc.sync.dma_start(out=out_v[e][:, t, 0:1024], in_=st[:, 0:1024])
-                nc.sync.dma_start(out=out_v[e][:, t, 1024:2048], in_=st[:, 1024:2048])
-            else:
-                nc.sync.dma_start(out=out_v[e][:, t, :], in_=st[:])
+            pieces = 4 if (e, t) == rows[-1] else 2
+            width = O // pieces
+            for k in range(pieces):
+                nc.sync.dma_start(
+                    out=out_v[e][:, t, k * width : (k + 1) * width],
+                    in_=st[:, k * width : (k + 1) * width],
+                )
             if (e, t) == (0, 5):
                 transposes([("G", 0, 1, 0), ("G", 1, 1, 0)], False)
             if (e, t) == (1, 1):

@@ -78,6 +78,12 @@ def tile_flaxparallelexperts_kernel(tc, inputs, weight, expert_size, grad_out, o
         nc.vector.memset(warm_in[:], 0.0)
         nc.scalar.copy(out=warm_out[:], in_=warm_in[:])
 
+        def copy_out(engine, dst, src):
+            if engine == "A":
+                nc.scalar.copy(out=dst, in_=src)
+            else:
+                nc.vector.tensor_copy(out=dst, in_=src)
+
         def quantise(u, grp):
             nm = u[0] + ("%d" * (len(u) - 1)) % tuple(u[1:])
             cd = keep.tile([P, NT], U32, name="cd" + nm, align_bytes=64)
@@ -90,31 +96,33 @@ def tile_flaxparallelexperts_kernel(tc, inputs, weight, expert_size, grad_out, o
             codes[u] = cd
             scales[u] = sc
 
-        def transposes(units, quantise_each):
-            grps = []
+        def transposes(units):
+            grp = {}
             for u in units:
-                grp = grpp.tile([P, 4 * NT], BF16, name="grp", tag="grp", align_bytes=64)
-                grp_w = grp[:].bitcast(F32)
-                for b in range(2):
-                    tp = psum.tile([P, NT], F32, name="tp", tag="bank")
-                    for j in range(4):
-                        nc.tensor.transpose(
-                            out=tp[:, j * P : (j + 1) * P],
-                            in_=raw[u][:, (4 * b + j) * P : (4 * b + j + 1) * P],
-                            identity=ident[:],
-                        )
-                    dst = grp_w[:, b * NT : (b + 1) * NT].rearrange("k (t p u) -> k t p u", t=2, u=2)
-                    src = tp[:].rearrange("k (t u p) -> k t p u", t=2, u=2)
-                    if b == 0:
-                        nc.vector.tensor_copy(out=dst, in_=src)
-                    else:
-                        nc.scalar.copy(out=dst, in_=src)
-                if quantise_each:
-                    quantise(u, grp)
+                grp[u] = grpp.tile([P, 4 * NT], BF16, name="grp", tag="grp", align_bytes=64)
+            if units[0][0] == "X":
+                order = [(u, b) for b in range(2) for u in units]
+            else:
+                order = [(u, b) for u in units for b in range(2)]
+            for u, b in order:
+                tp = psum.tile([P, NT], F32, name="tp", tag="bank")
+                for j in range(4):
+                    nc.tensor.transpose(
+                        out=tp[:, j * P : (j + 1) * P],
+                        in_=raw[u][:, (4 * b + j) * P : (4 * b + j + 1) * P],
+                        identity=ident[:],
+                    )
+                words = grp[u][:].bitcast(F32)
+                if u[0] == "X":
+                    dst = words.rearrange("k (p b w) -> k b p w", b=2, w=4)[:, b]
+                    src = tp[:].rearrange("k (w p) -> k p w", w=4)
+                    copy_out("AD"[u[1]], dst, src)
                 else:
-                    grps.append((u, grp))
-            for u, grp in grps:
-                quantise(u, grp)
+                    dst = words[:, b * NT : (b + 1) * NT].rearrange("k (t p u) -> k t p u", t=2, u=2)
+                    src = tp[:].rearrange("k (t u p) -> k t p u", t=2, u=2)
+                    copy_out("DA"[b], dst, src)
+            for u in units:
+                quantise(u, grp[u])
 
         first = [const.tile([P, 4, 2 * NT], F32, name="first%d" % half) for half in range(2)]
         stage = {}
@@ -147,12 +155,7 @@ def tile_flaxparallelexperts_kernel(tc, inputs, weight, expert_size, grad_out, o
                     stop=(c == C - 1),
                 )
             for k, (e, t, ch) in enumerate(tiles):
-                dst = stage_of(e, t, ch).rearrange("i (p t) -> i p t", t=4)
-                src = accs[k][:].rearrange("i (t p) -> i p t", t=4)
-                if pattern[k] == "A":
-                    nc.scalar.copy(out=dst, in_=src)
-                else:
-                    nc.vector.tensor_copy(out=dst, in_=src)
+                copy_out(pattern[k], stage_of(e, t, ch), accs[k][:])
 
         out_v = [out[e].rearrange("(p t) o -> p t o", t=8) for e in range(E)]
 
@@ -162,33 +165,32 @@ def tile_flaxparallelexperts_kernel(tc, inputs, weight, expert_size, grad_out, o
         def row_quad(e, t):
             return [(e, t, ch) for ch in range(4)]
 
-        transposes([("X", 0, 0)], True)
-        transposes([("X", 1, 0)], True)
-        transposes([("G", 0, 0, 0)], True)
-        transposes([("G", 1, 0, 0)], True)
+        transposes([("X", 0, 0)])
+        transposes([("X", 1, 0)])
+        transposes([("G", 0, 0, 0)])
+        transposes([("G", 1, 0, 0)])
         products(column_quad(0, 0, 0), "ADAA", True)
-        transposes([("X", 0, 1), ("X", 1, 1)], False)
-        transposes([("X", 0, 2), ("X", 1, 2)], False)
-        products(column_quad(0, 0, 1), "ADAA", False)
+        transposes([("X", 0, 1), ("X", 1, 1)])
+        transposes([("X", 0, 2), ("X", 1, 2)])
+        products(column_quad(0, 0, 1), "ADAA", True)
         nc.sync.dma_start(out=out_v[0][:, 0:4, 0:1024], in_=first[0][:])
-        transposes([("X", 0, 3), ("X", 1, 3)], False)
-        products(column_quad(0, 0, 2), "ADAA", False)
-        transposes([("G", 0, 0, 1), ("G", 1, 0, 1)], False)
-        products(column_quad(0, 0, 3), "ADAA", False)
+        transposes([("X", 0, 3), ("X", 1, 3)])
+        products(column_quad(0, 0, 2), "ADAA", True)
+        transposes([("G", 0, 0, 1), ("G", 1, 0, 1)])
+        products(column_quad(0, 0, 3), "ADAA", True)
         nc.sync.dma_start(out=out_v[0][:, 0:4, 1024:2048], in_=first[1][:])
 
         rows = [(0, t) for t in range(4, 8)] + [(1, t) for t in range(8)]
         for e, t in rows:
-            products(row_quad(e, t), "ADAD", False)
+            last = (e, t) == rows[-1]
+            products(row_quad(e, t), "ADAD", not last)
             st = stage[(e, t)]
-            pieces = 4 if (e, t) == rows[-1] else 2
-            width = O // pieces
-            for k in range(pieces):
-                nc.sync.dma_start(
-                    out=out_v[e][:, t, k * width : (k + 1) * width],
-                    in_=st[:, k * width : (k + 1) * width],
-                )
+            if last:
+                nc.sync.dma_start(out=out_v[e][:, t, 0:1024], in_=st[:, 0:1024])
+                nc.sync.dma_start(out=out_v[e][:, t, 1024:2048], in_=st[:, 1024:2048])
+            else:
+                nc.sync.dma_start(out=out_v[e][:, t, :], in_=st[:])
             if (e, t) == (0, 5):
-                transposes([("G", 0, 1, 0), ("G", 1, 1, 0)], False)
+                transposes([("G", 0, 1, 0), ("G", 1, 1, 0)])
             if (e, t) == (1, 1):
-                transposes([("G", 0, 1, 1), ("G", 1, 1, 1)], False)
+                transposes([("G", 0, 1, 1), ("G", 1, 1, 1)])

@@ -34,42 +34,49 @@ def tile_flaxparallelexperts_kernel(tc, inputs, weight, expert_size, grad_out, o
         ctx.enter_context(tc.manual_schedule())
 
         raw = {}
+        grouped = {}
         codes = {}
         scales = {}
 
+        def name_of(u):
+            return "%s%d%d%d" % u
+
+        def load(src, rows_a_partition, units):
+            lo = units[0][2]
+            hi = units[-1][2] + units[-1][3]
+            t = rawp.tile([P, (hi - lo) * 2 * N], BF16, name="raw" + name_of(units[0]))
+            nc.sync.dma_start(
+                out=t[:],
+                in_=src.rearrange("(p t) n -> p (t n)", t=rows_a_partition)[:, (lo % 4) * 2 * N : (lo % 4 + hi - lo) * 2 * N],
+            )
+            for u in units:
+                raw[u] = t[:].bitcast(F32)[:, (u[2] - lo) * NT : (u[2] - lo + u[3]) * NT]
+
+        def x_unit(c, ch):
+            return ("X", c, 2 * ch, 2)
+
         def load_x(c, ch):
-            t = rawp.tile([P, 4 * N], BF16, name="xr%d%d" % (c, ch))
+            t = rawp.tile([P, 4 * N], BF16, name="raw" + name_of(x_unit(c, ch)))
             nc.sync.dma_start(
-                out=t[:],
-                in_=inputs[c, ch * 512 : (ch + 1) * 512, :].rearrange("(p t) n -> p (t n)", t=4),
+                out=t[:], in_=inputs[c, ch * 512 : (ch + 1) * 512, :].rearrange("(p t) n -> p (t n)", t=4)
             )
-            raw[("X", c, ch)] = t[:].bitcast(F32)
+            raw[x_unit(c, ch)] = t[:].bitcast(F32)
 
-        def load_g_half(c, e, h):
-            t = rawp.tile([P, 4 * N], BF16, name="gr%d%d%d" % (c, e, h))
-            nc.sync.dma_start(
-                out=t[:],
-                in_=grad_out[c * E + e].rearrange("(p t) n -> p (t n)", t=8)[:, h * 4 * N : (h + 1) * 4 * N],
-            )
-            raw[("G", c, e, h)] = t[:].bitcast(F32)
-
-        def load_g_whole(c, e):
-            t = rawp.tile([P, 8 * N], BF16, name="gr%d%d" % (c, e))
-            nc.sync.dma_start(out=t[:], in_=grad_out[c * E + e].rearrange("(p t) n -> p (t n)", t=8))
-            for h in range(2):
-                raw[("G", c, e, h)] = t[:].bitcast(F32)[:, h * 2 * N : (h + 1) * 2 * N]
+        def load_g(units):
+            load(grad_out[units[0][1]], 8, units)
 
         load_x(0, 0)
         load_x(1, 0)
-        load_g_half(0, 0, 0)
-        load_g_half(1, 0, 0)
+        for b in range(2):
+            for c in range(C):
+                load_g([("G", c * E, b, 1)])
         for ch in range(1, 4):
             load_x(0, ch)
             load_x(1, ch)
-        load_g_half(0, 0, 1)
-        load_g_half(1, 0, 1)
-        load_g_whole(0, 1)
-        load_g_whole(1, 1)
+        for c in range(C):
+            load_g([("G", c * E, 2, 2)])
+        for c in range(C):
+            load_g([("G", c * E + 1, 0, 2), ("G", c * E + 1, 2, 2)])
 
         ident = const.tile([P, P], F32, name="ident")
         make_identity(nc, ident[:])
@@ -84,45 +91,36 @@ def tile_flaxparallelexperts_kernel(tc, inputs, weight, expert_size, grad_out, o
             else:
                 nc.vector.tensor_copy(out=dst, in_=src)
 
-        def quantise(u, grp):
-            nm = u[0] + ("%d" * (len(u) - 1)) % tuple(u[1:])
-            cd = keep.tile([P, NT], U32, name="cd" + nm, align_bytes=64)
-            sc = keep.tile([P, NT], U8, name="sc" + nm, align_bytes=64)
-            nc.vector.quantize_mx(
-                out=cd[:].bitcast(E4M3X4 if u[0] == "X" else E5M2X4),
-                scales=sc[:],
-                in_=grp[:],
-            )
-            codes[u] = cd
-            scales[u] = sc
-
-        def transposes(units):
-            grp = {}
+        def transposes(units, engines):
+            k = 0
             for u in units:
-                grp[u] = grpp.tile([P, 4 * NT], BF16, name="grp", tag="grp", align_bytes=64)
-            if units[0][0] == "X":
-                order = [(u, b) for b in range(2) for u in units]
-            else:
-                order = [(u, b) for u in units for b in range(2)]
-            for u, b in order:
-                tp = psum.tile([P, NT], F32, name="tp", tag="bank")
-                for j in range(4):
-                    nc.tensor.transpose(
-                        out=tp[:, j * P : (j + 1) * P],
-                        in_=raw[u][:, (4 * b + j) * P : (4 * b + j + 1) * P],
-                        identity=ident[:],
+                banks = u[3]
+                grouped[u] = grpp.tile(
+                    [P, banks * 2 * NT], BF16, name="grp%d" % banks, tag="grp%d" % banks, align_bytes=64
+                )
+                for b in range(banks):
+                    tp = psum.tile([P, NT], F32, name="tp", tag="bank")
+                    for j in range(4):
+                        nc.tensor.transpose(
+                            out=tp[:, j * P : (j + 1) * P],
+                            in_=raw[u][:, (4 * b + j) * P : (4 * b + j + 1) * P],
+                            identity=ident[:],
+                        )
+                    copy_out(
+                        engines[k],
+                        grouped[u][:].bitcast(F32)[:, b * NT : (b + 1) * NT].rearrange("k (t p u) -> k t p u", t=2, u=2),
+                        tp[:].rearrange("k (t u p) -> k t p u", t=2, u=2),
                     )
-                words = grp[u][:].bitcast(F32)
-                if u[0] == "X":
-                    dst = words.rearrange("k (p b w) -> k b p w", b=2, w=4)[:, b]
-                    src = tp[:].rearrange("k (w p) -> k p w", w=4)
-                    copy_out("AD"[u[1]], dst, src)
-                else:
-                    dst = words[:, b * NT : (b + 1) * NT].rearrange("k (t p u) -> k t p u", t=2, u=2)
-                    src = tp[:].rearrange("k (t u p) -> k t p u", t=2, u=2)
-                    copy_out("DA"[b], dst, src)
+                    k += 1
             for u in units:
-                quantise(u, grp[u])
+                banks = u[3]
+                codes[u] = keep.tile([P, banks * NT // 2], U32, name="cd" + name_of(u), align_bytes=64)
+                scales[u] = keep.tile([P, banks * NT // 2], U8, name="sc" + name_of(u), align_bytes=64)
+                nc.vector.quantize_mx(
+                    out=codes[u][:].bitcast(E4M3X4 if u[0] == "X" else E5M2X4),
+                    scales=scales[u][:],
+                    in_=grouped[u][:],
+                )
 
         first = [const.tile([P, 4, 2 * NT], F32, name="first%d" % half) for half in range(2)]
         stage = {}
@@ -134,17 +132,18 @@ def tile_flaxparallelexperts_kernel(tc, inputs, weight, expert_size, grad_out, o
                 stage[(e, t)] = stgp.tile([P, O], F32, name="stg", tag="stg")
             return stage[(e, t)][:, ch * NT : (ch + 1) * NT]
 
-        def products(tiles, pattern, chunk_major):
+        def g_unit(c, e, t):
+            if e == 0 and t < 4:
+                return ("G", c * E, t // 2, 1), t % 2
+            return ("G", c * E + e, 2 * (t // 4), 2), t % 4
+
+        def products(tiles, pattern, order):
             accs = [psum.tile([P, NT], F32, name="acc", tag="bank") for tl in tiles]
-            if chunk_major:
-                order = [(c, k) for c in range(C) for k in range(len(tiles))]
-            else:
-                order = [(c, k) for k in range(len(tiles)) for c in range(C)]
             for c, k in order:
                 e, t, ch = tiles[k]
-                g = ("G", c, e, t // 4)
-                x = ("X", c, ch)
-                cols = slice((t % 4) * P, (t % 4 + 1) * P)
+                g, block = g_unit(c, e, t)
+                x = x_unit(c, ch)
+                cols = slice(block * P, (block + 1) * P)
                 nc.tensor.matmul_mx(
                     out=accs[k][:],
                     lhsT=codes[g][:, cols].bitcast(E5M2X4),
@@ -155,35 +154,50 @@ def tile_flaxparallelexperts_kernel(tc, inputs, weight, expert_size, grad_out, o
                     stop=(c == C - 1),
                 )
             for k, (e, t, ch) in enumerate(tiles):
-                copy_out(pattern[k], stage_of(e, t, ch), accs[k][:])
+                copy_out(
+                    pattern[k],
+                    stage_of(e, t, ch).rearrange("i (p t) -> i p t", t=4),
+                    accs[k][:].rearrange("i (t p) -> i p t", t=4),
+                )
+
+        chunk_major = [(c, k) for c in range(C) for k in range(4)]
+        tile_major = [(c, k) for k in range(4) for c in range(C)]
+        pair_major = [(c, 2 * b + k) for b in range(2) for c in range(C) for k in range(2)]
 
         out_v = [out[e].rearrange("(p t) o -> p t o", t=8) for e in range(E)]
 
-        def column_quad(e, h, ch):
-            return [(e, 4 * h + tt, ch) for tt in range(4)]
+        def column_quad(ch):
+            return [(0, t, ch) for t in range(4)]
 
         def row_quad(e, t):
             return [(e, t, ch) for ch in range(4)]
 
-        transposes([("X", 0, 0)])
-        transposes([("X", 1, 0)])
-        transposes([("G", 0, 0, 0)])
-        transposes([("G", 1, 0, 0)])
-        products(column_quad(0, 0, 0), "ADAA", True)
-        transposes([("X", 0, 1), ("X", 1, 1)])
-        transposes([("X", 0, 2), ("X", 1, 2)])
-        products(column_quad(0, 0, 1), "ADAA", True)
+        def x_pair(ch):
+            return [x_unit(c, ch) for c in range(C)]
+
+        def g_pair(e, h):
+            return [("G", c * E + e, 2 * h, 2) for c in range(C)]
+
+        transposes([x_unit(0, 0)], "DA")
+        transposes([x_unit(1, 0)], "DA")
+        for b in range(2):
+            for c in range(C):
+                transposes([("G", c * E, b, 1)], "A")
+        products(column_quad(0), "ADAA", pair_major)
+        transposes(x_pair(1), "DADA")
+        transposes(x_pair(2), "DADA")
+        products(column_quad(1), "ADAA", chunk_major)
         nc.sync.dma_start(out=out_v[0][:, 0:4, 0:1024], in_=first[0][:])
-        transposes([("X", 0, 3), ("X", 1, 3)])
-        products(column_quad(0, 0, 2), "ADAA", True)
-        transposes([("G", 0, 0, 1), ("G", 1, 0, 1)])
-        products(column_quad(0, 0, 3), "ADAA", True)
+        transposes(x_pair(3), "DADA")
+        products(column_quad(2), "ADAA", chunk_major)
+        transposes(g_pair(0, 1), "DADA")
+        products(column_quad(3), "ADAA", chunk_major)
         nc.sync.dma_start(out=out_v[0][:, 0:4, 1024:2048], in_=first[1][:])
 
         rows = [(0, t) for t in range(4, 8)] + [(1, t) for t in range(8)]
         for e, t in rows:
             last = (e, t) == rows[-1]
-            products(row_quad(e, t), "ADAD", not last)
+            products(row_quad(e, t), "ADAD", tile_major if last else chunk_major)
             st = stage[(e, t)]
             if last:
                 nc.sync.dma_start(out=out_v[e][:, t, 0:1024], in_=st[:, 0:1024])
@@ -191,6 +205,6 @@ def tile_flaxparallelexperts_kernel(tc, inputs, weight, expert_size, grad_out, o
             else:
                 nc.sync.dma_start(out=out_v[e][:, t, :], in_=st[:])
             if (e, t) == (0, 5):
-                transposes([("G", 0, 1, 0), ("G", 1, 1, 0)])
+                transposes(g_pair(1, 0), "DADA")
             if (e, t) == (1, 1):
-                transposes([("G", 0, 1, 1), ("G", 1, 1, 1)])
+                transposes(g_pair(1, 1), "DADA")

@@ -85,6 +85,14 @@ def tile_flaxparallelexperts_kernel(tc, inputs, weight, expert_size, grad_out, o
         nc.vector.memset(warm_in[:], 0.0)
         nc.scalar.copy(out=warm_out[:], in_=warm_in[:])
 
+        zeros = const.tile([P, NT], BF16, name="zeros")
+        nc.vector.memset(zeros[:], 0.0)
+
+        def idle_passes(n):
+            idle = psum.tile([P, NT], F32, name="idle", tag="bank")
+            for r in range(n):
+                nc.tensor.matmul(out=idle[:], lhsT=zeros[:, 0:P], rhs=zeros[:], start=True, stop=True)
+
         def copy_out(engine, dst, src):
             if engine == "A":
                 nc.scalar.copy(out=dst, in_=src)
@@ -178,11 +186,15 @@ def tile_flaxparallelexperts_kernel(tc, inputs, weight, expert_size, grad_out, o
         def g_pair(e, h):
             return [("G", c * E + e, 2 * h, 2) for c in range(C)]
 
+        idle_passes(8)
         transposes([x_unit(0, 0)], "DA")
+        idle_passes(2)
         transposes([x_unit(1, 0)], "DA")
+        idle_passes(1)
         for b in range(2):
             for c in range(C):
                 transposes([("G", c * E, b, 1)], "A")
+                idle_passes(1)
         products(column_quad(0), "ADAA", pair_major)
         transposes(x_pair(1), "DADA")
         transposes(x_pair(2), "DADA")

@@ -41,42 +41,41 @@ def tile_flaxparallelexperts_kernel(tc, inputs, weight, expert_size, grad_out, o
         def name_of(u):
             return "%s%d%d%d" % u
 
-        def load(src, rows_a_partition, units):
-            lo = units[0][2]
+        def load(units):
+            kind, m, lo = units[0][0:3]
             hi = units[-1][2] + units[-1][3]
+            if kind == "X":
+                ch = lo // 2
+                rows = inputs[m, ch * 512 : (ch + 1) * 512, :].rearrange("(p t) n -> p (t n)", t=4)
+                base = 2 * ch
+            else:
+                rows = grad_out[m].rearrange("(p t) n -> p (t n)", t=8)
+                base = 0
             t = rawp.tile([P, (hi - lo) * 2 * N], BF16, name="raw" + name_of(units[0]))
-            nc.sync.dma_start(
-                out=t[:],
-                in_=src.rearrange("(p t) n -> p (t n)", t=rows_a_partition)[:, (lo % 4) * 2 * N : (lo % 4 + hi - lo) * 2 * N],
-            )
+            nc.sync.dma_start(out=t[:], in_=rows[:, (lo - base) * 2 * N : (hi - base) * 2 * N])
             for u in units:
                 raw[u] = t[:].bitcast(F32)[:, (u[2] - lo) * NT : (u[2] - lo + u[3]) * NT]
 
         def x_unit(c, ch):
             return ("X", c, 2 * ch, 2)
 
-        def load_x(c, ch):
-            t = rawp.tile([P, 4 * N], BF16, name="raw" + name_of(x_unit(c, ch)))
-            nc.sync.dma_start(
-                out=t[:], in_=inputs[c, ch * 512 : (ch + 1) * 512, :].rearrange("(p t) n -> p (t n)", t=4)
-            )
-            raw[x_unit(c, ch)] = t[:].bitcast(F32)
+        def x_pair(ch):
+            return [x_unit(c, ch) for c in range(C)]
 
-        def load_g(units):
-            load(grad_out[units[0][1]], 8, units)
+        def g_pair(e, h):
+            return [("G", c * E + e, 2 * h, 2) for c in range(C)]
 
-        load_x(0, 0)
-        load_x(1, 0)
-        for b in range(2):
-            for c in range(C):
-                load_g([("G", c * E, b, 1)])
-        for ch in range(1, 4):
-            load_x(0, ch)
-            load_x(1, ch)
+        pieces = []
         for c in range(C):
-            load_g([("G", c * E, 2, 2)])
+            pieces += [("X", c, 0, 1), ("X", c, 1, 1), ("G", c * E, 0, 1)]
+        pieces += [("G", c * E, 1, 1) for c in range(C)]
+
+        for u in pieces:
+            load([u])
+        for u in x_pair(1) + x_pair(2) + x_pair(3) + g_pair(0, 1):
+            load([u])
         for c in range(C):
-            load_g([("G", c * E + 1, 0, 2), ("G", c * E + 1, 2, 2)])
+            load([g_pair(1, 0)[c], g_pair(1, 1)[c]])
 
         ident = const.tile([P, P], F32, name="ident")
         make_identity(nc, ident[:])
@@ -85,19 +84,23 @@ def tile_flaxparallelexperts_kernel(tc, inputs, weight, expert_size, grad_out, o
         nc.vector.memset(warm_in[:], 0.0)
         nc.scalar.copy(out=warm_out[:], in_=warm_in[:])
 
-        zeros = const.tile([P, NT], BF16, name="zeros")
-        nc.vector.memset(zeros[:], 0.0)
-
-        def idle_passes(n):
-            idle = psum.tile([P, NT], F32, name="idle", tag="bank")
-            for r in range(n):
-                nc.tensor.matmul(out=idle[:], lhsT=zeros[:, 0:P], rhs=zeros[:], start=True, stop=True)
-
         def copy_out(engine, dst, src):
             if engine == "A":
                 nc.scalar.copy(out=dst, in_=src)
             else:
                 nc.vector.tensor_copy(out=dst, in_=src)
+
+        def quantise(u):
+            home = x_unit(u[1], u[2] // 2) if u[0] == "X" else u
+            if home not in codes:
+                codes[home] = keep.tile([P, home[3] * NT // 2], U32, name="cd" + name_of(home), align_bytes=64)
+                scales[home] = keep.tile([P, home[3] * NT // 2], U8, name="sc" + name_of(home), align_bytes=64)
+            cols = slice((u[2] - home[2]) * NT // 2, (u[2] - home[2] + u[3]) * NT // 2)
+            nc.vector.quantize_mx(
+                out=codes[home][:, cols].bitcast(E4M3X4 if u[0] == "X" else E5M2X4),
+                scales=scales[home][:, cols],
+                in_=grouped[u][:],
+            )
 
         def transposes(units, engines):
             k = 0
@@ -121,14 +124,7 @@ def tile_flaxparallelexperts_kernel(tc, inputs, weight, expert_size, grad_out, o
                     )
                     k += 1
             for u in units:
-                banks = u[3]
-                codes[u] = keep.tile([P, banks * NT // 2], U32, name="cd" + name_of(u), align_bytes=64)
-                scales[u] = keep.tile([P, banks * NT // 2], U8, name="sc" + name_of(u), align_bytes=64)
-                nc.vector.quantize_mx(
-                    out=codes[u][:].bitcast(E4M3X4 if u[0] == "X" else E5M2X4),
-                    scales=scales[u][:],
-                    in_=grouped[u][:],
-                )
+                quantise(u)
 
         first = [const.tile([P, 4, 2 * NT], F32, name="first%d" % half) for half in range(2)]
         stage = {}
@@ -180,22 +176,9 @@ def tile_flaxparallelexperts_kernel(tc, inputs, weight, expert_size, grad_out, o
         def row_quad(e, t):
             return [(e, t, ch) for ch in range(4)]
 
-        def x_pair(ch):
-            return [x_unit(c, ch) for c in range(C)]
-
-        def g_pair(e, h):
-            return [("G", c * E + e, 2 * h, 2) for c in range(C)]
-
-        idle_passes(8)
-        transposes([x_unit(0, 0)], "DA")
-        idle_passes(2)
-        transposes([x_unit(1, 0)], "DA")
-        idle_passes(1)
-        for b in range(2):
-            for c in range(C):
-                transposes([("G", c * E, b, 1)], "A")
-                idle_passes(1)
-        products(column_quad(0), "ADAA", pair_major)
+        for u, engine in zip(pieces, "ADAADAAA"):
+            transposes([u], engine)
+        products(column_quad(0), "DADA", pair_major)
         transposes(x_pair(1), "DADA")
         transposes(x_pair(2), "DADA")
         products(column_quad(1), "ADAA", chunk_major)

@@ -31,7 +31,6 @@ def tile_flaxparallelexperts_kernel(tc, inputs, weight, expert_size, grad_out, o
         keep = ctx.enter_context(tc.tile_pool(name="keep", bufs=1))
         stgp = ctx.enter_context(tc.tile_pool(name="stg", bufs=8))
         psum = ctx.enter_context(tc.psum_pool(name="psum", bufs=8))
-        ctx.enter_context(tc.manual_schedule())
 
         raw = {}
         grouped = {}
@@ -41,41 +40,42 @@ def tile_flaxparallelexperts_kernel(tc, inputs, weight, expert_size, grad_out, o
         def name_of(u):
             return "%s%d%d%d" % u
 
-        def load(units):
-            kind, m, lo = units[0][0:3]
+        def load(src, rows_a_partition, units):
+            lo = units[0][2]
             hi = units[-1][2] + units[-1][3]
-            if kind == "X":
-                ch = lo // 2
-                rows = inputs[m, ch * 512 : (ch + 1) * 512, :].rearrange("(p t) n -> p (t n)", t=4)
-                base = 2 * ch
-            else:
-                rows = grad_out[m].rearrange("(p t) n -> p (t n)", t=8)
-                base = 0
             t = rawp.tile([P, (hi - lo) * 2 * N], BF16, name="raw" + name_of(units[0]))
-            nc.sync.dma_start(out=t[:], in_=rows[:, (lo - base) * 2 * N : (hi - base) * 2 * N])
+            nc.sync.dma_start(
+                out=t[:],
+                in_=src.rearrange("(p t) n -> p (t n)", t=rows_a_partition)[:, (lo % 4) * 2 * N : (lo % 4 + hi - lo) * 2 * N],
+            )
             for u in units:
                 raw[u] = t[:].bitcast(F32)[:, (u[2] - lo) * NT : (u[2] - lo + u[3]) * NT]
 
         def x_unit(c, ch):
             return ("X", c, 2 * ch, 2)
 
-        def x_pair(ch):
-            return [x_unit(c, ch) for c in range(C)]
+        def load_x(c, ch):
+            t = rawp.tile([P, 4 * N], BF16, name="raw" + name_of(x_unit(c, ch)))
+            nc.sync.dma_start(
+                out=t[:], in_=inputs[c, ch * 512 : (ch + 1) * 512, :].rearrange("(p t) n -> p (t n)", t=4)
+            )
+            raw[x_unit(c, ch)] = t[:].bitcast(F32)
 
-        def g_pair(e, h):
-            return [("G", c * E + e, 2 * h, 2) for c in range(C)]
+        def load_g(units):
+            load(grad_out[units[0][1]], 8, units)
 
-        pieces = []
+        load_x(0, 0)
+        load_x(1, 0)
+        for b in range(2):
+            for c in range(C):
+                load_g([("G", c * E, b, 1)])
+        for ch in range(1, 4):
+            load_x(0, ch)
+            load_x(1, ch)
         for c in range(C):
-            pieces += [("X", c, 0, 1), ("X", c, 1, 1), ("G", c * E, 0, 1)]
-        pieces += [("G", c * E, 1, 1) for c in range(C)]
-
-        for u in pieces:
-            load([u])
-        for u in x_pair(1) + x_pair(2) + x_pair(3) + g_pair(0, 1):
-            load([u])
+            load_g([("G", c * E, 2, 2)])
         for c in range(C):
-            load([g_pair(1, 0)[c], g_pair(1, 1)[c]])
+            load_g([("G", c * E + 1, 0, 2), ("G", c * E + 1, 2, 2)])
 
         ident = const.tile([P, P], F32, name="ident")
         make_identity(nc, ident[:])
@@ -89,18 +89,6 @@ def tile_flaxparallelexperts_kernel(tc, inputs, weight, expert_size, grad_out, o
                 nc.scalar.copy(out=dst, in_=src)
             else:
                 nc.vector.tensor_copy(out=dst, in_=src)
-
-        def quantise(u):
-            home = x_unit(u[1], u[2] // 2) if u[0] == "X" else u
-            if home not in codes:
-                codes[home] = keep.tile([P, home[3] * NT // 2], U32, name="cd" + name_of(home), align_bytes=64)
-                scales[home] = keep.tile([P, home[3] * NT // 2], U8, name="sc" + name_of(home), align_bytes=64)
-            cols = slice((u[2] - home[2]) * NT // 2, (u[2] - home[2] + u[3]) * NT // 2)
-            nc.vector.quantize_mx(
-                out=codes[home][:, cols].bitcast(E4M3X4 if u[0] == "X" else E5M2X4),
-                scales=scales[home][:, cols],
-                in_=grouped[u][:],
-            )
 
         def transposes(units, engines):
             k = 0
@@ -124,7 +112,14 @@ def tile_flaxparallelexperts_kernel(tc, inputs, weight, expert_size, grad_out, o
                     )
                     k += 1
             for u in units:
-                quantise(u)
+                banks = u[3]
+                codes[u] = keep.tile([P, banks * NT // 2], U32, name="cd" + name_of(u), align_bytes=64)
+                scales[u] = keep.tile([P, banks * NT // 2], U8, name="sc" + name_of(u), align_bytes=64)
+                nc.vector.quantize_mx(
+                    out=codes[u][:].bitcast(E4M3X4 if u[0] == "X" else E5M2X4),
+                    scales=scales[u][:],
+                    in_=grouped[u][:],
+                )
 
         first = [const.tile([P, 4, 2 * NT], F32, name="first%d" % half) for half in range(2)]
         stage = {}
@@ -176,9 +171,18 @@ def tile_flaxparallelexperts_kernel(tc, inputs, weight, expert_size, grad_out, o
         def row_quad(e, t):
             return [(e, t, ch) for ch in range(4)]
 
-        for u, engine in zip(pieces, "ADAADAAA"):
-            transposes([u], engine)
-        products(column_quad(0), "DADA", pair_major)
+        def x_pair(ch):
+            return [x_unit(c, ch) for c in range(C)]
+
+        def g_pair(e, h):
+            return [("G", c * E + e, 2 * h, 2) for c in range(C)]
+
+        transposes([x_unit(0, 0)], "DA")
+        transposes([x_unit(1, 0)], "DA")
+        for b in range(2):
+            for c in range(C):
+                transposes([("G", c * E, b, 1)], "A")
+        products(column_quad(0), "ADAA", pair_major)
         transposes(x_pair(1), "DADA")
         transposes(x_pair(2), "DADA")
         products(column_quad(1), "ADAA", chunk_major)

from contextlib import ExitStack

import concourse.mybir as mybir
from concourse.masks import make_identity

F32 = mybir.dt.float32
BF16 = mybir.dt.bfloat16
U32 = mybir.dt.uint32
U8 = mybir.dt.uint8
E4M3X4 = mybir.dt.float8_e4m3fn_x4
E5M2X4 = mybir.dt.float8_e5m2_x4

P = 128
C = 2
E = 2
I = 1024
O = 2048
N = 512
NT = 512

FLOPS = 2 * E * I * O * C * N
BYTES = 2 * (C * O * N + C * E * I * N) + 4 * E * I * O


def tile_flaxparallelexperts_kernel(tc, inputs, weight, expert_size, grad_out, out):
    nc = tc.nc
    with ExitStack() as ctx:
        const = ctx.enter_context(tc.tile_pool(name="const", bufs=1))
        rawp = ctx.enter_context(tc.tile_pool(name="raw", bufs=1))
        grpp = ctx.enter_context(tc.tile_pool(name="grp", bufs=4))
        keep = ctx.enter_context(tc.tile_pool(name="keep", bufs=1))
        stgp = ctx.enter_context(tc.tile_pool(name="stg", bufs=8))
        psum = ctx.enter_context(tc.psum_pool(name="psum", bufs=8))

        raw = {}
        grouped = {}
        codes = {}
        scales = {}

        def name_of(u):
            return "%s%d%d%d" % u

        def load(src, rows_a_partition, units):
            lo = units[0][2]
            hi = units[-1][2] + units[-1][3]
            t = rawp.tile([P, (hi - lo) * 2 * N], BF16, name="raw" + name_of(units[0]))
            nc.sync.dma_start(
                out=t[:],
                in_=src.rearrange("(p t) n -> p (t n)", t=rows_a_partition)[:, (lo % 4) * 2 * N : (lo % 4 + hi - lo) * 2 * N],
            )
            for u in units:
                raw[u] = t[:].bitcast(F32)[:, (u[2] - lo) * NT : (u[2] - lo + u[3]) * NT]

        def x_unit(c, ch):
            return ("X", c, 2 * ch, 2)

        def load_x(c, ch):
            t = rawp.tile([P, 4 * N], BF16, name="raw" + name_of(x_unit(c, ch)))
            nc.sync.dma_start(
                out=t[:], in_=inputs[c, ch * 512 : (ch + 1) * 512, :].rearrange("(p t) n -> p (t n)", t=4)
            )
            raw[x_unit(c, ch)] = t[:].bitcast(F32)

        def load_g(units):
            load(grad_out[units[0][1]], 8, units)

        load_x(0, 0)
        load_x(1, 0)
        for b in range(2):
            for c in range(C):
                load_g([("G", c * E, b, 1)])
        for ch in range(1, 4):
            load_x(0, ch)
            load_x(1, ch)
        for c in range(C):
            load_g([("G", c * E, 2, 2)])
        for c in range(C):
            load_g([("G", c * E + 1, 0, 2), ("G", c * E + 1, 2, 2)])

        ident = const.tile([P, P], F32, name="ident")
        make_identity(nc, ident[:])
        warm_in = const.tile([P, 8], F32, name="warm_in")
        warm_out = const.tile([P, 8], F32, name="warm_out")
        nc.vector.memset(warm_in[:], 0.0)
        nc.scalar.copy(out=warm_out[:], in_=warm_in[:])

        def copy_out(engine, dst, src):
            if engine == "A":
                nc.scalar.copy(out=dst, in_=src)
            else:
                nc.vector.tensor_copy(out=dst, in_=src)

        def transposes(units, engines):
            k = 0
            for u in units:
                banks = u[3]
                grouped[u] = grpp.tile(
                    [P, banks * 2 * NT], BF16, name="grp%d" % banks, tag="grp%d" % banks, align_bytes=64
                )
                for b in range(banks):
                    tp = psum.tile([P, NT], F32, name="tp", tag="bank")
                    for j in range(4):
                        nc.tensor.transpose(
                            out=tp[:, j * P : (j + 1) * P],
                            in_=raw[u][:, (4 * b + j) * P : (4 * b + j + 1) * P],
                            identity=ident[:],
                        )
                    copy_out(
                        engines[k],
                        grouped[u][:].bitcast(F32)[:, b * NT : (b + 1) * NT].rearrange("k (t p u) -> k t p u", t=2, u=2),
                        tp[:].rearrange("k (t u p) -> k t p u", t=2, u=2),
                    )
                    k += 1
            for u in units:
                banks = u[3]
                codes[u] = keep.tile([P, banks * NT // 2], U32, name="cd" + name_of(u), align_bytes=64)
                scales[u] = keep.tile([P, banks * NT // 2], U8, name="sc" + name_of(u), align_bytes=64)
                nc.vector.quantize_mx(
                    out=codes[u][:].bitcast(E4M3X4 if u[0] == "X" else E5M2X4),
                    scales=scales[u][:],
                    in_=grouped[u][:],
                )

        first = [const.tile([P, 4, 2 * NT], F32, name="first%d" % half) for half in range(2)]
        stage = {}

        def stage_of(e, t, ch):
            if e == 0 and t < 4:
                return first[ch // 2][:, t, (ch % 2) * NT : (ch % 2 + 1) * NT]
            if (e, t) not in stage:
                stage[(e, t)] = stgp.tile([P, O], F32, name="stg", tag="stg")
            return stage[(e, t)][:, ch * NT : (ch + 1) * NT]

        def g_unit(c, e, t):
            if e == 0 and t < 4:
                return ("G", c * E, t // 2, 1), t % 2
            return ("G", c * E + e, 2 * (t // 4), 2), t % 4

        def products(tiles, pattern, order):
            accs = [psum.tile([P, NT], F32, name="acc", tag="bank") for tl in tiles]
            for c, k in order:
                e, t, ch = tiles[k]
                g, block = g_unit(c, e, t)
                x = x_unit(c, ch)
                cols = slice(block * P, (block + 1) * P)
                nc.tensor.matmul_mx(
                    out=accs[k][:],
                    lhsT=codes[g][:, cols].bitcast(E5M2X4),
                    lhsT_scale=scales[g][:, cols],
                    rhs=codes[x][:].bitcast(E4M3X4),
                    rhs_scale=scales[x][:],
                    start=(c == 0),
                    stop=(c == C - 1),
                )
            for k, (e, t, ch) in enumerate(tiles):
                copy_out(
                    pattern[k],
                    stage_of(e, t, ch).rearrange("i (p t) -> i p t", t=4),
                    accs[k][:].rearrange("i (t p) -> i p t", t=4),
                )

        chunk_major = [(c, k) for c in range(C) for k in range(4)]
        tile_major = [(c, k) for k in range(4) for c in range(C)]
        pair_major = [(c, 2 * b + k) for b in range(2) for c in range(C) for k in range(2)]

        out_v = [out[e].rearrange("(p t) o -> p t o", t=8) for e in range(E)]

        def column_quad(ch):
            return [(0, t, ch) for t in range(4)]

        def row_quad(e, t):
            return [(e, t, ch) for ch in range(4)]

        def x_pair(ch):
            return [x_unit(c, ch) for c in range(C)]

        def g_pair(e, h):
            return [("G", c * E + e, 2 * h, 2) for c in range(C)]

        transposes([x_unit(0, 0)], "DA")
        transposes([x_unit(1, 0)], "DA")
        for b in range(2):
            for c in range(C):
                transposes([("G", c * E, b, 1)], "A")
        products(column_quad(0), "ADAA", pair_major)
        transposes(x_pair(1), "DADA")
        transposes(x_pair(2), "DADA")
        products(column_quad(1), "ADAA", chunk_major)
        nc.sync.dma_start(out=out_v[0][:, 0:4, 0:1024], in_=first[0][:])
        transposes(x_pair(3), "DADA")
        products(column_quad(2), "ADAA", chunk_major)
        transposes(g_pair(0, 1), "DADA")
        products(column_quad(3), "ADAA", chunk_major)
        nc.sync.dma_start(out=out_v[0][:, 0:4, 1024:2048], in_=first[1][:])

        rows = [(0, t) for t in range(4, 8)] + [(1, t) for t in range(8)]
        for e, t in rows:
            last = (e, t) == rows[-1]
            products(row_quad(e, t), "ADAD", tile_major if last else chunk_major)
            st = stage[(e, t)]
            if last:
                nc.sync.dma_start(out=out_v[e][:, t, 0:1024], in_=st[:, 0:1024])
                nc.sync.dma_start(out=out_v[e][:, t, 1024:2048], in_=st[:, 1024:2048])
            else:
                nc.sync.dma_start(out=out_v[e][:, t, :], in_=st[:])
            if (e, t) == (0, 5):
                transposes(g_pair(1, 0), "DADA")
            if (e, t) == (1, 1):
                transposes(g_pair(1, 1), "DADA")
